import numpy as np
import ml_dtypes


def mxq(x, axis, fmt="e4m3"):
    dtype, down = {"e4m3": (ml_dtypes.float8_e4m3fn, 7), "e5m2": (ml_dtypes.float8_e5m2, 14)}[fmt]
    v = np.moveaxis(np.asarray(x, np.float32).astype(ml_dtypes.bfloat16).astype(np.float64), axis, -1)
    blocks = v.reshape(v.shape[:-1] + (-1, 32))
    amax = np.abs(blocks).max(-1, keepdims=True)
    byte = np.maximum(np.where(amax > 0, np.frexp(amax)[1] - 1 + 127, 0) - down, 1)
    scale = np.exp2(byte - 127.0)
    codes = (blocks / scale).astype(np.float32).astype(dtype).astype(np.float64)
    return np.moveaxis((codes * scale).reshape(v.shape), -1, axis)


WIDE = False


def mx_kscale(k):
    if not WIDE:
        return np.ones(k)
    levels = np.array([10, -10, 5, -5, 0])
    if k % 512:
        return np.exp2(np.random.permutation(np.resize(levels, k // 32))).repeat(32)
    a = np.empty((k // 512, 16))
    for p in range(k // 512):
        a[p, :8] = np.random.permutation(np.resize(levels, 8))
        for g in range(8):
            far = levels[np.abs(levels - a[p, g]) >= 10]
            a[p, g + 8] = far[np.random.randint(len(far))]
    return np.exp2(a.ravel()).repeat(32)


BF16 = ml_dtypes.bfloat16


def bf(x):
    return np.asarray(x, np.float32).astype(BF16)


def f64(x):
    return np.asarray(x).astype(np.float64)


B, N, P, D, H = 2, 512, 4, 256, 8
E = P * D
DH = E // H


def sincos_table(n, e):
    pe = np.zeros((n, e))
    position = np.arange(n, dtype=np.float64)[:, None]
    div_term = np.exp(np.arange(0, e, 2, dtype=np.float64) * -(np.log(10000.0) / e))
    pe[:, 0::2] = np.sin(position * div_term)
    pe[:, 1::2] = np.cos(position * div_term)
    pe = pe - pe.mean()
    return pe / (pe.std() * 10)


def setup_inputs():
    s, t = mx_kscale(E), mx_kscale(E)
    c = 1.0 / np.sqrt(E)
    return {"x": bf(np.random.standard_normal((B, N, P, D)) * s.reshape(P, D)),
            "pos_embed": bf(sincos_table(N, E) * t),
            "W_embed": bf(np.random.standard_normal((E, E)) * c * t[:, None] / s),
            "b_embed": bf(np.random.standard_normal(E) * 0.1 * t),
            "Wq": bf(np.random.standard_normal((E, E)) * c / t),
            "bq": bf(np.random.standard_normal(E) * 0.1),
            "Wk": bf(np.random.standard_normal((E, E)) * c / t),
            "bk": bf(np.random.standard_normal(E) * 0.1),
            "Wv": bf(np.random.standard_normal((E, E)) * c / t),
            "bv": bf(np.random.standard_normal(E) * 0.1)}


def reference(x, pos_embed, W_embed, b_embed, Wq, bq, Wk, bk, Wv, bv):
    xf = f64(x).reshape(B, N, E)
    xe = (mxq(xf, 2, "e4m3") @ mxq(f64(W_embed).T, 0, "e4m3")) + f64(b_embed)
    xe = xe + f64(pos_embed)
    xq = mxq(xe, 2, "e4m3")
    q = ((xq @ mxq(f64(Wq).T, 0, "e4m3")) + f64(bq)).reshape(B, N, H, DH)
    k = ((xq @ mxq(f64(Wk).T, 0, "e4m3")) + f64(bk)).reshape(B, N, H, DH)
    v = ((xq @ mxq(f64(Wv).T, 0, "e4m3")) + f64(bv)).reshape(B, N, H, DH)
    return q, k, v

@@ -1,0 +1,318 @@
+from contextlib import ExitStack
+
+import concourse.mybir as mybir
+from concourse.masks import make_identity
+
+BF16 = mybir.dt.bfloat16
+F32 = mybir.dt.float32
+U32 = mybir.dt.uint32
+U8 = mybir.dt.uint8
+FP8X4 = mybir.dt.float8_e4m3fn_x4
+ADD = mybir.AluOpType.add
+IDENTITY = mybir.ActivationFunctionType.Identity
+
+P = 128
+PACK = 4
+K_PASS = P * PACK
+E = 1024
+PASSES = E // K_PASS
+POSITIONS = 512
+TOKENS = 2 * POSITIONS
+ROW_TILES = 8
+PAIRS = ROW_TILES // 2
+HALF = ROW_TILES // 2
+WORDS = E // 2
+BANK = 512
+LANE_TOKENS = 4
+
+FLOPS = 4 * 2 * TOKENS * E * E
+
+
+def transpose_pair(nc, psum, stage, raw, pair, ident):
+    raw_words = raw[:].bitcast(F32)
+    banks = []
+    for g in range(PASSES):
+        bank = psum.tile([P, 2, 2, P], F32, tag="bank")
+        for i in range(2):
+            for u in range(2):
+                first_word = (2 * pair + i) * WORDS + 2 * g * P + u
+                nc.tensor.transpose(
+                    bank[:, i, u, :], raw_words[:, first_word : first_word + 2 * P - 1 : 2], ident[:]
+                )
+        banks.append(bank)
+    grouped_tiles = []
+    for bank in banks:
+        grouped = stage.tile([P, 2 * P * PACK], BF16, tag="grouped", align_bytes=64)
+        nc.scalar.copy(
+            out=grouped[:].bitcast(F32).rearrange("p (i r u) -> p i r u", i=2, u=2),
+            in_=bank[:].rearrange("p i u r -> p i r u"),
+        )
+        grouped_tiles.append(grouped)
+    return grouped_tiles
+
+
+def quantise_pair(nc, grouped_tiles, pair, codes, scales):
+    cols = slice(2 * pair * P, 2 * (pair + 1) * P)
+    for g in range(PASSES):
+        nc.vector.quantize_mx(
+            out=codes[:, g, cols].bitcast(FP8X4), scales=scales[:, g, cols], in_=grouped_tiles[g][:]
+        )
+
+
+def tile_attention_pa_kernel(
+    tc, x, pos_embed, W_embed, b_embed, Wq, bq, Wk, bk, Wv, bv, out_0, out_1, out_2
+):
+    nc = tc.nc
+    weights = (Wq, Wk, Wv)
+    biases = (bq, bk, bv)
+
+    x_view = x.rearrange("b (r j) s d -> b r (j s d)", j=LANE_TOKENS)
+    pos_view = pos_embed.rearrange("(r j) e -> r j e", j=LANE_TOKENS)
+    out_views = [
+        out.rearrange("b (r j) h d -> b j r (h d)", j=LANE_TOKENS) for out in (out_0, out_1, out_2)
+    ]
+    w_embed_view = W_embed.rearrange("(g r t) k -> r g (t k)", r=P, t=PACK)
+    weight_views = [w.rearrange("(i r) k -> r i k", r=P) for w in weights]
+
+    with ExitStack() as ctx:
+        consts = ctx.enter_context(tc.tile_pool(name="consts", bufs=1))
+        raws = ctx.enter_context(tc.tile_pool(name="raws", bufs=3))
+        keep = ctx.enter_context(tc.tile_pool(name="keep", bufs=1))
+        stage = ctx.enter_context(tc.tile_pool(name="stage", bufs=8))
+        outs = ctx.enter_context(tc.tile_pool(name="outs", bufs=6))
+        psum = ctx.enter_context(tc.psum_pool(name="psum", bufs=8))
+        ctx.enter_context(tc.manual_schedule())
+
+        ident = consts.tile([P, P], F32)
+        make_identity(nc, ident[:])
+        ones = consts.tile([P, P], BF16)
+        nc.vector.memset(ones[:], 1.0)
+        bias_rows = consts.tile([P, 3 * E], BF16)
+        nc.vector.memset(bias_rows[:], 0.0)
+        b_embed_bf = consts.tile([P, PASSES, PACK], BF16)
+        nc.scalar.dma_start(
+            out=b_embed_bf[:], in_=b_embed.rearrange("(g r t) -> r g t", r=P, t=PACK)
+        )
+        b_embed_f32 = consts.tile([P, ROW_TILES], F32)
+        nc.scalar.activation(
+            out=b_embed_f32[:], in_=b_embed_bf[:].rearrange("p g t -> p (g t)"), func=IDENTITY
+        )
+
+        w_embed_raw = raws.tile([P, ROW_TILES * E], BF16, tag="raw")
+        x_raw = raws.tile([P, ROW_TILES * E], BF16, tag="raw")
+        wq_raw = raws.tile([P, ROW_TILES * E], BF16, tag="raw")
+        pos_raw = consts.tile([P, LANE_TOKENS, E], BF16)
+
+        def load_w_embed(pair):
+            g, u = divmod(pair, 2)
+            nc.sync.dma_start(
+                out=w_embed_raw[:, 2 * pair * E : 2 * (pair + 1) * E],
+                in_=w_embed_view[:, g, 2 * u * E : 2 * (u + 1) * E],
+            )
+
+        def load_x(pair):
+            b, half = divmod(pair, 2)
+            nc.sync.dma_start(
+                out=x_raw[:, 2 * pair * E : 2 * (pair + 1) * E],
+                in_=x_view[b][:, 2 * half * E : 2 * (half + 1) * E],
+            )
+
+        def load_pos(g_out):
+            cols = slice(g_out * K_PASS, (g_out + 1) * K_PASS)
+            nc.sync.dma_start(out=pos_raw[:, :, cols], in_=pos_view[:, :, cols])
+
+        def load_weight(raw, w):
+            for half in range(2):
+                tiles = slice(half * HALF, (half + 1) * HALF)
+                nc.sync.dma_start(
+                    out=raw[:].rearrange("p (i k) -> p i k", i=ROW_TILES)[:, tiles, :],
+                    in_=weight_views[w][:, tiles, :],
+                )
+
+        load_w_embed(0)
+        load_w_embed(1)
+        load_x(0)
+        load_x(1)
+        load_pos(0)
+        load_x(2)
+        load_x(3)
+        load_w_embed(2)
+        load_w_embed(3)
+        load_pos(1)
+        for w, bias in enumerate(biases):
+            nc.sync.dma_start(
+                out=bias_rows[0:1, w * E : (w + 1) * E], in_=bias.rearrange("(o f) -> o f", o=1)
+            )
+        load_weight(wq_raw, 0)
+
+        def mx_operand(name):
+            codes = keep.tile([P, PASSES, E], U32, name=name + "_codes", align_bytes=64)
+            scales = keep.tile([P, PASSES, E], U8, name=name + "_scales", align_bytes=64)
+            return codes, scales
+
+        x_mx = mx_operand("x")
+        we_mx = mx_operand("w_embed")
+        xe_mx = mx_operand("xe")
+        w_mx = [mx_operand(name) for name in ("wq", "wk", "wv")]
+
+        def transpose(raw, pairs):
+            return {pair: transpose_pair(nc, psum, stage, raw, pair, ident) for pair in pairs}
+
+        def quantise(grouped, operand):
+            for pair in sorted(grouped):
+                quantise_pair(nc, grouped[pair], pair, operand[0], operand[1])
+
+        pos_planes = consts.tile([P, ROW_TILES, POSITIONS], F32)
+
+        def transpose_pos(g_out):
+            for u in range(2):
+                first_word = 2 * g_out * P + u
+                bank = psum.tile([P, LANE_TOKENS, P], F32, tag="bank")
+                for j in range(LANE_TOKENS):
+                    nc.tensor.transpose(
+                        bank[:, j, :],
+                        pos_raw[:, j, :].bitcast(F32)[:, first_word : first_word + 2 * P - 1 : 2],
+                        ident[:],
+                    )
+                pairs = (
+                    bank[:]
+                    .rearrange("p j r -> p (j r)")
+                    .bitcast(BF16)
+                    .rearrange("p (c e) -> p c e", e=2)
+                )
+                for e in range(2):
+                    plane = PACK * g_out + 2 * u + e
+                    if u == 0:
+                        nc.scalar.activation(
+                            out=pos_planes[:, plane, :],
+                            in_=pairs[:, :, e],
+                            func=IDENTITY,
+                            bias=b_embed_f32[:, plane : plane + 1],
+                            scale=1.0,
+                        )
+                    else:
+                        nc.vector.tensor_scalar(
+                            out=pos_planes[:, plane, :],
+                            in0=pairs[:, :, e],
+                            scalar1=b_embed_f32[:, plane : plane + 1],
+                            scalar2=None,
+                            op0=ADD,
+                        )
+
+        xe_grouped = keep.tile([P, PASSES, TOKENS * PACK], BF16, align_bytes=64)
+
+        def embed(g_out, b):
+            for j in range(LANE_TOKENS):
+                first_token = (LANE_TOKENS * b + j) * P
+                tokens = slice(first_token, first_token + P)
+                acc = psum.tile([P, PACK, P], F32, tag="bank")
+                for t in range(PACK):
+                    features = slice((PACK * g_out + t) * P, (PACK * g_out + t + 1) * P)
+                    for g in range(PASSES):
+                        nc.tensor.matmul_mx(
+                            out=acc[:, t, :],
+                            lhsT=we_mx[0][:, g, features].bitcast(FP8X4),
+                            lhsT_scale=we_mx[1][:, g, features],
+                            rhs=x_mx[0][:, g, tokens].bitcast(FP8X4),
+                            rhs_scale=x_mx[1][:, g, tokens],
+                            start=(g == 0),
+                            stop=(g == PASSES - 1),
+                        )
+                nc.vector.tensor_tensor(
+                    out=xe_grouped[
+                        :, g_out, first_token * PACK : (first_token + P) * PACK
+                    ].rearrange("p (r t) -> p r t", t=PACK),
+                    in0=acc[:].rearrange("p t r -> p r t"),
+                    in1=pos_planes[
+                        :, PACK * g_out : PACK * (g_out + 1), j * P : (j + 1) * P
+                    ].rearrange("p t r -> p r t"),
+                    op=ADD,
+                )
+            batch = slice(b * POSITIONS, (b + 1) * POSITIONS)
+            nc.vector.quantize_mx(
+                out=xe_mx[0][:, g_out, batch].bitcast(FP8X4),
+                scales=xe_mx[1][:, g_out, batch],
+                in_=xe_grouped[:, g_out, b * POSITIONS * PACK : (b + 1) * POSITIONS * PACK],
+            )
+
+        bias_all = consts.tile([P, 3 * E], F32)
+
+        def spread_bias(w):
+            for h in range(E // BANK):
+                cols = slice(w * E + h * BANK, w * E + (h + 1) * BANK)
+                spread = psum.tile([P, BANK], F32, tag="bank")
+                nc.tensor.matmul(
+                    spread[:], lhsT=ones[:], rhs=bias_rows[:, cols], start=True, stop=True
+                )
+                nc.scalar.copy(out=bias_all[:, cols], in_=spread[:])
+
+        def project(w, tile_index):
+            codes, scales = w_mx[w]
+            tokens = slice(tile_index * P, (tile_index + 1) * P)
+            result = outs.tile([P, E], F32, tag="result")
+            for h in range(E // BANK):
+                features = slice(h * BANK, (h + 1) * BANK)
+                bias = bias_all[:, w * E + h * BANK : w * E + (h + 1) * BANK]
+                acc = psum.tile([P, BANK], F32, tag="bank")
+                for g in range(PASSES):
+                    nc.tensor.matmul_mx(
+                        out=acc[:],
+                        lhsT=xe_mx[0][:, g, tokens].bitcast(FP8X4),
+                        lhsT_scale=xe_mx[1][:, g, tokens],
+                        rhs=codes[:, g, features].bitcast(FP8X4),
+                        rhs_scale=scales[:, g, features],
+                        start=(g == 0),
+                        stop=(g == PASSES - 1),
+                    )
+                bank_number = (w * ROW_TILES + tile_index) * (E // BANK) + h
+                if bank_number % 3 == 0:
+                    nc.scalar.copy(out=result[:, features], in_=acc[:])
+                    nc.gpsimd.tensor_tensor(
+                        out=result[:, features], in0=result[:, features], in1=bias, op=ADD
+                    )
+                else:
+                    nc.vector.tensor_tensor(out=result[:, features], in0=acc[:], in1=bias, op=ADD)
+            b, j = divmod(tile_index, LANE_TOKENS)
+            nc.sync.dma_start(out=out_views[w][b, j], in_=result[:])
+
+        for pair in (0, 1):
+            quantise(transpose(w_embed_raw, [pair]), we_mx)
+        for pair in (0, 1):
+            quantise(transpose(x_raw, [pair]), x_mx)
+        transpose_pos(0)
+        x_grouped = transpose(x_raw, [2])
+        embed(0, 0)
+        quantise(x_grouped, x_mx)
+
+        x_grouped = transpose(x_raw, [3])
+        we_grouped = transpose(w_embed_raw, [2, 3])
+        quantise(x_grouped, x_mx)
+        quantise(we_grouped, we_mx)
+        later_raws = {}
+        for w in (1, 2):
+            later_raws[w] = raws.tile([P, ROW_TILES * E], BF16, tag="raw", name="later_raw")
+            load_weight(later_raws[w], w)
+        embed(0, 1)
+
+        transpose_pos(1)
+        wq_grouped = transpose(wq_raw, [0, 1])
+        embed(1, 0)
+        quantise(wq_grouped, w_mx[0])
+
+        wq_grouped = transpose(wq_raw, [2, 3])
+        spread_bias(0)
+        quantise(wq_grouped, w_mx[0])
+        embed(1, 1)
+
+        for step in range(PAIRS):
+            w = 1 + step // 2
+            half = step % 2
+            w_grouped = transpose(later_raws[w], [2 * half, 2 * half + 1])
+            project(0, 2 * step)
+            project(0, 2 * step + 1)
+            quantise(w_grouped, w_mx[w])
+            if half == 1:
+                spread_bias(w)
+        for w in (1, 2):
+            for tile_index in range(ROW_TILES):
+                project(w, tile_index)

@@ -20,7 +20,6 @@ POSITIONS = 512
 TOKENS = 2 * POSITIONS
 ROW_TILES = 8
 PAIRS = ROW_TILES // 2
-HALF = ROW_TILES // 2
 WORDS = E // 2
 BANK = 512
 LANE_TOKENS = 4
@@ -28,42 +27,10 @@ LANE_TOKENS = 4
 FLOPS = 4 * 2 * TOKENS * E * E
 
 
-def transpose_pair(nc, psum, stage, raw, pair, ident):
-    raw_words = raw[:].bitcast(F32)
-    banks = []
-    for g in range(PASSES):
-        bank = psum.tile([P, 2, 2, P], F32, tag="bank")
-        for i in range(2):
-            for u in range(2):
-                first_word = (2 * pair + i) * WORDS + 2 * g * P + u
-                nc.tensor.transpose(
-                    bank[:, i, u, :], raw_words[:, first_word : first_word + 2 * P - 1 : 2], ident[:]
-                )
-        banks.append(bank)
-    grouped_tiles = []
-    for bank in banks:
-        grouped = stage.tile([P, 2 * P * PACK], BF16, tag="grouped", align_bytes=64)
-        nc.scalar.copy(
-            out=grouped[:].bitcast(F32).rearrange("p (i r u) -> p i r u", i=2, u=2),
-            in_=bank[:].rearrange("p i u r -> p i r u"),
-        )
-        grouped_tiles.append(grouped)
-    return grouped_tiles
-
-
-def quantise_pair(nc, grouped_tiles, pair, codes, scales):
-    cols = slice(2 * pair * P, 2 * (pair + 1) * P)
-    for g in range(PASSES):
-        nc.vector.quantize_mx(
-            out=codes[:, g, cols].bitcast(FP8X4), scales=scales[:, g, cols], in_=grouped_tiles[g][:]
-        )
-
-
 def tile_attention_pa_kernel(
     tc, x, pos_embed, W_embed, b_embed, Wq, bq, Wk, bk, Wv, bv, out_0, out_1, out_2
 ):
     nc = tc.nc
-    weights = (Wq, Wk, Wv)
     biases = (bq, bk, bv)
 
     x_view = x.rearrange("b (r j) s d -> b r (j s d)", j=LANE_TOKENS)
@@ -72,23 +39,20 @@ def tile_attention_pa_kernel(
         out.rearrange("b (r j) h d -> b j r (h d)", j=LANE_TOKENS) for out in (out_0, out_1, out_2)
     ]
     w_embed_view = W_embed.rearrange("(g r t) k -> r g (t k)", r=P, t=PACK)
-    weight_views = [w.rearrange("(i r) k -> r i k", r=P) for w in weights]
+    weight_views = [w.rearrange("(i r) k -> r i k", r=P) for w in (Wq, Wk, Wv)]
 
     with ExitStack() as ctx:
         consts = ctx.enter_context(tc.tile_pool(name="consts", bufs=1))
-        raws = ctx.enter_context(tc.tile_pool(name="raws", bufs=3))
+        raws = ctx.enter_context(tc.tile_pool(name="raws", bufs=16))
         keep = ctx.enter_context(tc.tile_pool(name="keep", bufs=1))
         stage = ctx.enter_context(tc.tile_pool(name="stage", bufs=8))
+        sums = ctx.enter_context(tc.tile_pool(name="sums", bufs=3))
         outs = ctx.enter_context(tc.tile_pool(name="outs", bufs=6))
         psum = ctx.enter_context(tc.psum_pool(name="psum", bufs=8))
         ctx.enter_context(tc.manual_schedule())
 
         ident = consts.tile([P, P], F32)
         make_identity(nc, ident[:])
-        ones = consts.tile([P, P], BF16)
-        nc.vector.memset(ones[:], 1.0)
-        bias_rows = consts.tile([P, 3 * E], BF16)
-        nc.vector.memset(bias_rows[:], 0.0)
         b_embed_bf = consts.tile([P, PASSES, PACK], BF16)
         nc.scalar.dma_start(
             out=b_embed_bf[:], in_=b_embed.rearrange("(g r t) -> r g t", r=P, t=PACK)
@@ -98,52 +62,45 @@ def tile_attention_pa_kernel(
             out=b_embed_f32[:], in_=b_embed_bf[:].rearrange("p g t -> p (g t)"), func=IDENTITY
         )
 
-        w_embed_raw = raws.tile([P, ROW_TILES * E], BF16, tag="raw")
-        x_raw = raws.tile([P, ROW_TILES * E], BF16, tag="raw")
-        wq_raw = raws.tile([P, ROW_TILES * E], BF16, tag="raw")
-        pos_raw = consts.tile([P, LANE_TOKENS, E], BF16)
-
         def load_w_embed(pair):
             g, u = divmod(pair, 2)
-            nc.sync.dma_start(
-                out=w_embed_raw[:, 2 * pair * E : 2 * (pair + 1) * E],
-                in_=w_embed_view[:, g, 2 * u * E : 2 * (u + 1) * E],
-            )
+            raw = raws.tile([P, 2 * E], BF16, tag="raw")
+            nc.sync.dma_start(out=raw[:], in_=w_embed_view[:, g, 2 * u * E : 2 * (u + 1) * E])
+            return raw
 
         def load_x(pair):
             b, half = divmod(pair, 2)
-            nc.sync.dma_start(
-                out=x_raw[:, 2 * pair * E : 2 * (pair + 1) * E],
-                in_=x_view[b][:, 2 * half * E : 2 * (half + 1) * E],
-            )
+            raw = raws.tile([P, 2 * E], BF16, tag="raw")
+            nc.sync.dma_start(out=raw[:], in_=x_view[b][:, 2 * half * E : 2 * (half + 1) * E])
+            return raw
 
         def load_pos(g_out):
-            cols = slice(g_out * K_PASS, (g_out + 1) * K_PASS)
-            nc.sync.dma_start(out=pos_raw[:, :, cols], in_=pos_view[:, :, cols])
-
-        def load_weight(raw, w):
-            for half in range(2):
-                tiles = slice(half * HALF, (half + 1) * HALF)
-                nc.sync.dma_start(
-                    out=raw[:].rearrange("p (i k) -> p i k", i=ROW_TILES)[:, tiles, :],
-                    in_=weight_views[w][:, tiles, :],
-                )
-
-        load_w_embed(0)
-        load_w_embed(1)
-        load_x(0)
-        load_x(1)
-        load_pos(0)
-        load_x(2)
-        load_x(3)
-        load_w_embed(2)
-        load_w_embed(3)
-        load_pos(1)
-        for w, bias in enumerate(biases):
+            raw = consts.tile([P, LANE_TOKENS, K_PASS], BF16, name="pos_raw_%d" % g_out)
             nc.sync.dma_start(
-                out=bias_rows[0:1, w * E : (w + 1) * E], in_=bias.rearrange("(o f) -> o f", o=1)
+                out=raw[:], in_=pos_view[:, :, g_out * K_PASS : (g_out + 1) * K_PASS]
             )
-        load_weight(wq_raw, 0)
+            return raw
+
+        def load_weight(w, pair):
+            raw = raws.tile([P, 2 * E], BF16, tag="raw")
+            nc.sync.dma_start(
+                out=raw[:].rearrange("p (i k) -> p i k", i=2),
+                in_=weight_views[w][:, 2 * pair : 2 * (pair + 1), :],
+            )
+            return raw
+
+        bias_all = consts.tile([P, 3, E], BF16)
+
+        w_embed_raw = [load_w_embed(0), load_w_embed(1)]
+        x_raw = [load_x(0)]
+        pos_raw = [load_pos(0)]
+        x_raw += [load_x(pair) for pair in (1, 2, 3)]
+        w_embed_raw += [load_w_embed(2), load_w_embed(3)]
+        pos_raw.append(load_pos(1))
+        weight_raw = [[load_weight(0, pair) for pair in range(PAIRS)]]
+        for w, bias in enumerate(biases):
+            nc.sync.dma_start(out=bias_all[:, w, :], in_=bias.partition_broadcast(P))
+        weight_raw += [[load_weight(w, pair) for pair in range(PAIRS)] for w in (1, 2)]
 
         def mx_operand(name):
             codes = keep.tile([P, PASSES, E], U32, name=name + "_codes", align_bytes=64)
@@ -155,24 +112,44 @@ def tile_attention_pa_kernel(
         xe_mx = mx_operand("xe")
         w_mx = [mx_operand(name) for name in ("wq", "wk", "wv")]
 
-        def transpose(raw, pairs):
-            return {pair: transpose_pair(nc, psum, stage, raw, pair, ident) for pair in pairs}
+        def transpose(raw):
+            words = raw[:].bitcast(F32)
+            grouped_tiles = []
+            for g in range(PASSES):
+                bank = psum.tile([P, 2, 2, P], F32, tag="bank")
+                for i in range(2):
+                    for u in range(2):
+                        first_word = i * WORDS + 2 * g * P + u
+                        nc.tensor.transpose(
+                            bank[:, i, u, :], words[:, first_word : first_word + 2 * P - 1 : 2], ident[:]
+                        )
+                grouped = stage.tile([P, 2 * P * PACK], BF16, tag="grouped", align_bytes=64)
+                nc.scalar.copy(
+                    out=grouped[:].bitcast(F32).rearrange("p (i r u) -> p i r u", i=2, u=2),
+                    in_=bank[:].rearrange("p i u r -> p i r u"),
+                )
+                grouped_tiles.append(grouped)
+            return grouped_tiles
 
-        def quantise(grouped, operand):
-            for pair in sorted(grouped):
-                quantise_pair(nc, grouped[pair], pair, operand[0], operand[1])
+        def quantise(grouped_tiles, pair, operand):
+            cols = slice(2 * pair * P, 2 * (pair + 1) * P)
+            for g in range(PASSES):
+                nc.vector.quantize_mx(
+                    out=operand[0][:, g, cols].bitcast(FP8X4),
+                    scales=operand[1][:, g, cols],
+                    in_=grouped_tiles[g][:],
+                )
 
-        pos_planes = consts.tile([P, ROW_TILES, POSITIONS], F32)
+        pos_planes = [
+            consts.tile([P, PACK, POSITIONS], F32, name="pos_planes_%d" % g) for g in range(PASSES)
+        ]
 
         def transpose_pos(g_out):
             for u in range(2):
-                first_word = 2 * g_out * P + u
                 bank = psum.tile([P, LANE_TOKENS, P], F32, tag="bank")
                 for j in range(LANE_TOKENS):
                     nc.tensor.transpose(
-                        bank[:, j, :],
-                        pos_raw[:, j, :].bitcast(F32)[:, first_word : first_word + 2 * P - 1 : 2],
-                        ident[:],
+                        bank[:, j, :], pos_raw[g_out][:, j, :].bitcast(F32)[:, u : 2 * P : 2], ident[:]
                     )
                 pairs = (
                     bank[:]
@@ -181,70 +158,54 @@ def tile_attention_pa_kernel(
                     .rearrange("p (c e) -> p c e", e=2)
                 )
                 for e in range(2):
-                    plane = PACK * g_out + 2 * u + e
-                    if u == 0:
-                        nc.scalar.activation(
-                            out=pos_planes[:, plane, :],
-                            in_=pairs[:, :, e],
-                            func=IDENTITY,
-                            bias=b_embed_f32[:, plane : plane + 1],
-                            scale=1.0,
-                        )
-                    else:
-                        nc.vector.tensor_scalar(
-                            out=pos_planes[:, plane, :],
-                            in0=pairs[:, :, e],
-                            scalar1=b_embed_f32[:, plane : plane + 1],
-                            scalar2=None,
-                            op0=ADD,
-                        )
+                    t = 2 * u + e
+                    feature_tile = PACK * g_out + t
+                    nc.scalar.activation(
+                        out=pos_planes[g_out][:, t, :],
+                        in_=pairs[:, :, e],
+                        func=IDENTITY,
+                        bias=b_embed_f32[:, feature_tile : feature_tile + 1],
+                        scale=1.0,
+                    )
 
-        xe_grouped = keep.tile([P, PASSES, TOKENS * PACK], BF16, align_bytes=64)
+        xe_sums = {}
 
-        def embed(g_out, b):
-            for j in range(LANE_TOKENS):
-                first_token = (LANE_TOKENS * b + j) * P
-                tokens = slice(first_token, first_token + P)
-                acc = psum.tile([P, PACK, P], F32, tag="bank")
-                for t in range(PACK):
-                    features = slice((PACK * g_out + t) * P, (PACK * g_out + t + 1) * P)
-                    for g in range(PASSES):
-                        nc.tensor.matmul_mx(
-                            out=acc[:, t, :],
-                            lhsT=we_mx[0][:, g, features].bitcast(FP8X4),
-                            lhsT_scale=we_mx[1][:, g, features],
-                            rhs=x_mx[0][:, g, tokens].bitcast(FP8X4),
-                            rhs_scale=x_mx[1][:, g, tokens],
-                            start=(g == 0),
-                            stop=(g == PASSES - 1),
-                        )
-                nc.vector.tensor_tensor(
-                    out=xe_grouped[
-                        :, g_out, first_token * PACK : (first_token + P) * PACK
-                    ].rearrange("p (r t) -> p r t", t=PACK),
-                    in0=acc[:].rearrange("p t r -> p r t"),
-                    in1=pos_planes[
-                        :, PACK * g_out : PACK * (g_out + 1), j * P : (j + 1) * P
-                    ].rearrange("p t r -> p r t"),
-                    op=ADD,
+        def embed(g_out, tile_index):
+            b, j = divmod(tile_index, LANE_TOKENS)
+            if j == 0:
+                xe_sums[g_out, b] = sums.tile(
+                    [P, POSITIONS * PACK], BF16, tag="xe_sum", name="xe_sum", align_bytes=64
                 )
+            tokens = slice(tile_index * P, (tile_index + 1) * P)
+            acc = psum.tile([P, PACK, P], F32, tag="bank")
+            for t in range(PACK):
+                features = slice((PACK * g_out + t) * P, (PACK * g_out + t + 1) * P)
+                for g in range(PASSES):
+                    nc.tensor.matmul_mx(
+                        out=acc[:, t, :],
+                        lhsT=we_mx[0][:, g, features].bitcast(FP8X4),
+                        lhsT_scale=we_mx[1][:, g, features],
+                        rhs=x_mx[0][:, g, tokens].bitcast(FP8X4),
+                        rhs_scale=x_mx[1][:, g, tokens],
+                        start=(g == 0),
+                        stop=(g == PASSES - 1),
+                    )
+            nc.vector.tensor_tensor(
+                out=xe_sums[g_out, b][:, j * P * PACK : (j + 1) * P * PACK].rearrange(
+                    "p (r t) -> p r t", t=PACK
+                ),
+                in0=acc[:].rearrange("p t r -> p r t"),
+                in1=pos_planes[g_out][:, :, j * P : (j + 1) * P].rearrange("p t r -> p r t"),
+                op=ADD,
+            )
+
+        def quantise_xe(g_out, b):
             batch = slice(b * POSITIONS, (b + 1) * POSITIONS)
             nc.vector.quantize_mx(
                 out=xe_mx[0][:, g_out, batch].bitcast(FP8X4),
                 scales=xe_mx[1][:, g_out, batch],
-                in_=xe_grouped[:, g_out, b * POSITIONS * PACK : (b + 1) * POSITIONS * PACK],
+                in_=xe_sums[g_out, b][:],
             )
-
-        bias_all = consts.tile([P, 3 * E], F32)
-
-        def spread_bias(w):
-            for h in range(E // BANK):
-                cols = slice(w * E + h * BANK, w * E + (h + 1) * BANK)
-                spread = psum.tile([P, BANK], F32, tag="bank")
-                nc.tensor.matmul(
-                    spread[:], lhsT=ones[:], rhs=bias_rows[:, cols], start=True, stop=True
-                )
-                nc.scalar.copy(out=bias_all[:, cols], in_=spread[:])
 
         def project(w, tile_index):
             codes, scales = w_mx[w]
@@ -252,7 +213,7 @@ def tile_attention_pa_kernel(
             result = outs.tile([P, E], F32, tag="result")
             for h in range(E // BANK):
                 features = slice(h * BANK, (h + 1) * BANK)
-                bias = bias_all[:, w * E + h * BANK : w * E + (h + 1) * BANK]
+                bias = bias_all[:, w, features]
                 acc = psum.tile([P, BANK], F32, tag="bank")
                 for g in range(PASSES):
                     nc.tensor.matmul_mx(
@@ -275,44 +236,43 @@ def tile_attention_pa_kernel(
             b, j = divmod(tile_index, LANE_TOKENS)
             nc.sync.dma_start(out=out_views[w][b, j], in_=result[:])
 
-        for pair in (0, 1):
-            quantise(transpose(w_embed_raw, [pair]), we_mx)
-        for pair in (0, 1):
-            quantise(transpose(x_raw, [pair]), x_mx)
+        w0 = transpose(w_embed_raw[0])
+        w1 = transpose(w_embed_raw[1])
+        quantise(w0, 0, we_mx)
+        x0 = transpose(x_raw[0])
+        quantise(w1, 1, we_mx)
         transpose_pos(0)
-        x_grouped = transpose(x_raw, [2])
-        embed(0, 0)
-        quantise(x_grouped, x_mx)
-
-        x_grouped = transpose(x_raw, [3])
-        we_grouped = transpose(w_embed_raw, [2, 3])
-        quantise(x_grouped, x_mx)
-        quantise(we_grouped, we_mx)
-        later_raws = {}
-        for w in (1, 2):
-            later_raws[w] = raws.tile([P, ROW_TILES * E], BF16, tag="raw", name="later_raw")
-            load_weight(later_raws[w], w)
-        embed(0, 1)
-
+        quantise(x0, 0, x_mx)
+        for pair in (1, 2, 3):
+            x_grouped = transpose(x_raw[pair])
+            embed(0, 2 * pair - 2)
+            embed(0, 2 * pair - 1)
+            quantise(x_grouped, pair, x_mx)
+            if pair == 2:
+                quantise_xe(0, 0)
+        w2 = transpose(w_embed_raw[2])
+        embed(0, 6)
+        embed(0, 7)
+        quantise(w2, 2, we_mx)
+        quantise_xe(0, 1)
+        w3 = transpose(w_embed_raw[3])
         transpose_pos(1)
-        wq_grouped = transpose(wq_raw, [0, 1])
-        embed(1, 0)
-        quantise(wq_grouped, w_mx[0])
+        quantise(w3, 3, we_mx)
+        for pair in range(PAIRS):
+            w_grouped = transpose(weight_raw[0][pair])
+            embed(1, 2 * pair)
+            embed(1, 2 * pair + 1)
+            quantise(w_grouped, pair, w_mx[0])
+            if pair == 1:
+                quantise_xe(1, 0)
+        quantise_xe(1, 1)
 
-        wq_grouped = transpose(wq_raw, [2, 3])
-        spread_bias(0)
-        quantise(wq_grouped, w_mx[0])
-        embed(1, 1)
-
-        for step in range(PAIRS):
-            w = 1 + step // 2
-            half = step % 2
-            w_grouped = transpose(later_raws[w], [2 * half, 2 * half + 1])
-            project(0, 2 * step)
-            project(0, 2 * step + 1)
-            quantise(w_grouped, w_mx[w])
-            if half == 1:
-                spread_bias(w)
-        for w in (1, 2):
+        for w in range(3):
             for tile_index in range(ROW_TILES):
+                pair, second = divmod(tile_index, 2)
+                ahead = w < 2 and not second
+                if ahead:
+                    w_grouped = transpose(weight_raw[w + 1][pair])
                 project(w, tile_index)
+                if ahead:
+                    quantise(w_grouped, pair, w_mx[w + 1])

@@ -43,8 +43,9 @@ def tile_attention_pa_kernel(
 
     with ExitStack() as ctx:
         consts = ctx.enter_context(tc.tile_pool(name="consts", bufs=1))
-        raws = ctx.enter_context(tc.tile_pool(name="raws", bufs=16))
+        raws = ctx.enter_context(tc.tile_pool(name="raws", bufs=14))
         keep = ctx.enter_context(tc.tile_pool(name="keep", bufs=1))
+        split = ctx.enter_context(tc.tile_pool(name="split", bufs=6))
         stage = ctx.enter_context(tc.tile_pool(name="stage", bufs=8))
         sums = ctx.enter_context(tc.tile_pool(name="sums", bufs=3))
         outs = ctx.enter_context(tc.tile_pool(name="outs", bufs=6))
@@ -97,10 +98,10 @@ def tile_attention_pa_kernel(
         x_raw += [load_x(pair) for pair in (1, 2, 3)]
         w_embed_raw += [load_w_embed(2), load_w_embed(3)]
         pos_raw.append(load_pos(1))
-        weight_raw = [[load_weight(0, pair) for pair in range(PAIRS)]]
+        weight_raw = [[load_weight(w, pair) for pair in range(PAIRS)] for w in (0, 1)]
         for w, bias in enumerate(biases):
             nc.sync.dma_start(out=bias_all[:, w, :], in_=bias.partition_broadcast(P))
-        weight_raw += [[load_weight(w, pair) for pair in range(PAIRS)] for w in (1, 2)]
+        weight_raw.append([load_weight(2, pair) for pair in range(PAIRS)])
 
         def mx_operand(name):
             codes = keep.tile([P, PASSES, E], U32, name=name + "_codes", align_bytes=64)
@@ -112,17 +113,30 @@ def tile_attention_pa_kernel(
         xe_mx = mx_operand("xe")
         w_mx = [mx_operand(name) for name in ("wq", "wk", "wv")]
 
-        def transpose(raw):
+        def split_words(raw):
+            sorted_words = split.tile([P, 2 * E], BF16, tag="split", name="sorted_words")
+            for i in range(2):
+                cols = slice(i * E, (i + 1) * E)
+                nc.gpsimd.tensor_copy(
+                    out=sorted_words[:, cols].bitcast(U32).rearrange("p (g u w) -> p g u w", g=2, u=2),
+                    in_=raw[:, cols].bitcast(U32).rearrange("p (g w u) -> p g u w", g=2, u=2),
+                )
+            return sorted_words
+
+        def transpose(raw, split=False):
             words = raw[:].bitcast(F32)
             grouped_tiles = []
             for g in range(PASSES):
                 bank = psum.tile([P, 2, 2, P], F32, tag="bank")
                 for i in range(2):
                     for u in range(2):
-                        first_word = i * WORDS + 2 * g * P + u
-                        nc.tensor.transpose(
-                            bank[:, i, u, :], words[:, first_word : first_word + 2 * P - 1 : 2], ident[:]
-                        )
+                        if split:
+                            first_word = i * WORDS + (2 * g + u) * P
+                            block = words[:, first_word : first_word + P]
+                        else:
+                            first_word = i * WORDS + 2 * g * P + u
+                            block = words[:, first_word : first_word + 2 * P - 1 : 2]
+                        nc.tensor.transpose(bank[:, i, u, :], block, ident[:])
                 grouped = stage.tile([P, 2 * P * PACK], BF16, tag="grouped", align_bytes=64)
                 nc.scalar.copy(
                     out=grouped[:].bitcast(F32).rearrange("p (i r u) -> p i r u", i=2, u=2),
@@ -236,6 +250,8 @@ def tile_attention_pa_kernel(
             b, j = divmod(tile_index, LANE_TOKENS)
             nc.sync.dma_start(out=out_views[w][b, j], in_=result[:])
 
+        w_split = {(w, pair): split_words(weight_raw[w][pair]) for w in (0, 1) for pair in range(PAIRS)}
+
         w0 = transpose(w_embed_raw[0])
         w1 = transpose(w_embed_raw[1])
         quantise(w0, 0, we_mx)
@@ -243,26 +259,33 @@ def tile_attention_pa_kernel(
         quantise(w1, 1, we_mx)
         transpose_pos(0)
         quantise(x0, 0, x_mx)
-        for pair in (1, 2, 3):
-            x_grouped = transpose(x_raw[pair])
-            embed(0, 2 * pair - 2)
-            embed(0, 2 * pair - 1)
-            quantise(x_grouped, pair, x_mx)
-            if pair == 2:
-                quantise_xe(0, 0)
+        x1 = transpose(x_raw[1])
+        embed(0, 0)
+        quantise(x1, 1, x_mx)
+        x2 = transpose(x_raw[2])
+        embed(0, 1)
+        embed(0, 2)
+        quantise(x2, 2, x_mx)
+        x3 = transpose(x_raw[3])
+        embed(0, 3)
+        embed(0, 4)
+        quantise(x3, 3, x_mx)
+        quantise_xe(0, 0)
         w2 = transpose(w_embed_raw[2])
-        embed(0, 6)
-        embed(0, 7)
+        embed(0, 5)
         quantise(w2, 2, we_mx)
-        quantise_xe(0, 1)
         w3 = transpose(w_embed_raw[3])
-        transpose_pos(1)
+        embed(0, 6)
         quantise(w3, 3, we_mx)
+        transpose_pos(1)
+        embed(0, 7)
         for pair in range(PAIRS):
-            w_grouped = transpose(weight_raw[0][pair])
+            w_grouped = transpose(w_split[0, pair], split=True)
             embed(1, 2 * pair)
             embed(1, 2 * pair + 1)
             quantise(w_grouped, pair, w_mx[0])
+            if pair == 0:
+                quantise_xe(0, 1)
             if pair == 1:
                 quantise_xe(1, 0)
         quantise_xe(1, 1)
@@ -272,7 +295,9 @@ def tile_attention_pa_kernel(
                 pair, second = divmod(tile_index, 2)
                 ahead = w < 2 and not second
                 if ahead:
-                    w_grouped = transpose(weight_raw[w + 1][pair])
+                    w_grouped = transpose(w_split[w + 1, pair], split=True)
                 project(w, tile_index)
                 if ahead:
                     quantise(w_grouped, pair, w_mx[w + 1])
+                elif w == 0:
+                    w_split[2, pair] = split_words(weight_raw[2][pair])

@@ -45,7 +45,7 @@ def tile_attention_pa_kernel(
         consts = ctx.enter_context(tc.tile_pool(name="consts", bufs=1))
         raws = ctx.enter_context(tc.tile_pool(name="raws", bufs=14))
         keep = ctx.enter_context(tc.tile_pool(name="keep", bufs=1))
-        split = ctx.enter_context(tc.tile_pool(name="split", bufs=6))
+        split = ctx.enter_context(tc.tile_pool(name="split", bufs=4))
         stage = ctx.enter_context(tc.tile_pool(name="stage", bufs=8))
         sums = ctx.enter_context(tc.tile_pool(name="sums", bufs=3))
         outs = ctx.enter_context(tc.tile_pool(name="outs", bufs=6))
@@ -113,14 +113,12 @@ def tile_attention_pa_kernel(
         xe_mx = mx_operand("xe")
         w_mx = [mx_operand(name) for name in ("wq", "wk", "wv")]
 
-        def split_words(raw):
+        def split_words(copy, raw):
             sorted_words = split.tile([P, 2 * E], BF16, tag="split", name="sorted_words")
-            for i in range(2):
-                cols = slice(i * E, (i + 1) * E)
-                nc.gpsimd.tensor_copy(
-                    out=sorted_words[:, cols].bitcast(U32).rearrange("p (g u w) -> p g u w", g=2, u=2),
-                    in_=raw[:, cols].bitcast(U32).rearrange("p (g w u) -> p g u w", g=2, u=2),
-                )
+            copy(
+                out=sorted_words[:].bitcast(F32).rearrange("p (a u w) -> p a u w", a=4, u=2),
+                in_=raw[:].bitcast(F32).rearrange("p (a w u) -> p a u w", a=4, u=2),
+            )
             return sorted_words
 
         def transpose(raw, split=False):
@@ -250,7 +248,10 @@ def tile_attention_pa_kernel(
             b, j = divmod(tile_index, LANE_TOKENS)
             nc.sync.dma_start(out=out_views[w][b, j], in_=result[:])
 
-        w_split = {(w, pair): split_words(weight_raw[w][pair]) for w in (0, 1) for pair in range(PAIRS)}
+        w_split = {}
+
+        def split_weight(copy, w, pair):
+            w_split[w, pair] = split_words(copy, weight_raw[w][pair])
 
         w0 = transpose(w_embed_raw[0])
         w1 = transpose(w_embed_raw[1])
@@ -274,11 +275,14 @@ def tile_attention_pa_kernel(
         w2 = transpose(w_embed_raw[2])
         embed(0, 5)
         quantise(w2, 2, we_mx)
+        split_weight(nc.vector.tensor_copy, 0, 0)
         w3 = transpose(w_embed_raw[3])
         embed(0, 6)
         quantise(w3, 3, we_mx)
+        split_weight(nc.vector.tensor_copy, 0, 1)
         transpose_pos(1)
         embed(0, 7)
+        split_weight(nc.vector.tensor_copy, 0, 2)
         for pair in range(PAIRS):
             w_grouped = transpose(w_split[0, pair], split=True)
             embed(1, 2 * pair)
@@ -288,6 +292,11 @@ def tile_attention_pa_kernel(
                 quantise_xe(0, 1)
             if pair == 1:
                 quantise_xe(1, 0)
+            if pair == 0:
+                split_weight(nc.vector.tensor_copy, 0, 3)
+            elif pair < 3:
+                copy = nc.vector.tensor_copy if pair == 1 else nc.scalar.copy
+                split_weight(copy, 1, pair - 1)
         quantise_xe(1, 1)
 
         for w in range(3):
@@ -299,5 +308,6 @@ def tile_attention_pa_kernel(
                 project(w, tile_index)
                 if ahead:
                     quantise(w_grouped, pair, w_mx[w + 1])
-                elif w == 0:
-                    w_split[2, pair] = split_words(weight_raw[2][pair])
+                    after_next = (w + 1) * PAIRS + pair + 2
+                    if after_next < 3 * PAIRS:
+                        split_weight(nc.scalar.copy, *divmod(after_next, PAIRS))

@@ -90,7 +90,10 @@ def tile_attention_pa_kernel(
             )
             return raw
 
-        bias_all = consts.tile([P, 3, E], BF16)
+        bias_all = [consts.tile([P, E], BF16, name="bias_%d" % w) for w in range(3)]
+
+        def load_bias(w):
+            nc.sync.dma_start(out=bias_all[w][:], in_=biases[w].partition_broadcast(P))
 
         w_embed_raw = [load_w_embed(0), load_w_embed(1)]
         x_raw = [load_x(0)]
@@ -98,10 +101,11 @@ def tile_attention_pa_kernel(
         x_raw += [load_x(pair) for pair in (1, 2, 3)]
         w_embed_raw += [load_w_embed(2), load_w_embed(3)]
         pos_raw.append(load_pos(1))
-        weight_raw = [[load_weight(w, pair) for pair in range(PAIRS)] for w in (0, 1)]
-        for w, bias in enumerate(biases):
-            nc.sync.dma_start(out=bias_all[:, w, :], in_=bias.partition_broadcast(P))
-        weight_raw.append([load_weight(2, pair) for pair in range(PAIRS)])
+        weight_raw = [[load_weight(0, pair) for pair in range(PAIRS)]]
+        load_bias(0)
+        weight_raw += [[load_weight(w, pair) for pair in range(PAIRS)] for w in (1, 2)]
+        load_bias(1)
+        load_bias(2)
 
         def mx_operand(name):
             codes = keep.tile([P, PASSES, E], U32, name=name + "_codes", align_bytes=64)
@@ -225,7 +229,7 @@ def tile_attention_pa_kernel(
             result = outs.tile([P, E], F32, tag="result")
             for h in range(E // BANK):
                 features = slice(h * BANK, (h + 1) * BANK)
-                bias = bias_all[:, w, features]
+                bias = bias_all[w][:, features]
                 acc = psum.tile([P, BANK], F32, tag="bank")
                 for g in range(PASSES):
                     nc.tensor.matmul_mx(
@@ -238,7 +242,11 @@ def tile_attention_pa_kernel(
                         stop=(g == PASSES - 1),
                     )
                 bank_number = (w * ROW_TILES + tile_index) * (E // BANK) + h
-                if bank_number % 3 == 0:
+                if w < 2:
+                    shared = bank_number % 4 == 3
+                else:
+                    shared = bank_number % 3 == 0
+                if shared:
                     nc.scalar.copy(out=result[:, features], in_=acc[:])
                     nc.gpsimd.tensor_tensor(
                         out=result[:, features], in0=result[:, features], in1=bias, op=ADD

@@ -48,7 +48,7 @@ def tile_attention_pa_kernel(
         split = ctx.enter_context(tc.tile_pool(name="split", bufs=4))
         stage = ctx.enter_context(tc.tile_pool(name="stage", bufs=8))
         sums = ctx.enter_context(tc.tile_pool(name="sums", bufs=3))
-        outs = ctx.enter_context(tc.tile_pool(name="outs", bufs=6))
+        outs = ctx.enter_context(tc.tile_pool(name="outs", bufs=12))
         psum = ctx.enter_context(tc.psum_pool(name="psum", bufs=8))
         ctx.enter_context(tc.manual_schedule())
 
@@ -101,8 +101,9 @@ def tile_attention_pa_kernel(
         x_raw += [load_x(pair) for pair in (1, 2, 3)]
         w_embed_raw += [load_w_embed(2), load_w_embed(3)]
         pos_raw.append(load_pos(1))
-        weight_raw = [[load_weight(0, pair) for pair in range(PAIRS)]]
+        weight_raw = [[load_weight(0, 0), load_weight(0, 1)]]
         load_bias(0)
+        weight_raw[0] += [load_weight(0, 2), load_weight(0, 3)]
         weight_raw += [[load_weight(w, pair) for pair in range(PAIRS)] for w in (1, 2)]
         load_bias(1)
         load_bias(2)
@@ -223,43 +224,44 @@ def tile_attention_pa_kernel(
                 in_=xe_sums[g_out, b][:],
             )
 
-        def project(w, tile_index):
+        def project(w, h, tile_index):
             codes, scales = w_mx[w]
-            tokens = slice(tile_index * P, (tile_index + 1) * P)
-            result = outs.tile([P, E], F32, tag="result")
-            for h in range(E // BANK):
-                features = slice(h * BANK, (h + 1) * BANK)
-                bias = bias_all[w][:, features]
-                acc = psum.tile([P, BANK], F32, tag="bank")
-                for g in range(PASSES):
-                    nc.tensor.matmul_mx(
-                        out=acc[:],
-                        lhsT=xe_mx[0][:, g, tokens].bitcast(FP8X4),
-                        lhsT_scale=xe_mx[1][:, g, tokens],
-                        rhs=codes[:, g, features].bitcast(FP8X4),
-                        rhs_scale=scales[:, g, features],
-                        start=(g == 0),
-                        stop=(g == PASSES - 1),
-                    )
-                bank_number = (w * ROW_TILES + tile_index) * (E // BANK) + h
-                if w < 2:
-                    shared = bank_number % 4 == 3
-                else:
-                    shared = bank_number % 3 == 0
-                if shared:
-                    nc.scalar.copy(out=result[:, features], in_=acc[:])
-                    nc.gpsimd.tensor_tensor(
-                        out=result[:, features], in0=result[:, features], in1=bias, op=ADD
-                    )
-                else:
-                    nc.vector.tensor_tensor(out=result[:, features], in0=acc[:], in1=bias, op=ADD)
             b, j = divmod(tile_index, LANE_TOKENS)
-            nc.sync.dma_start(out=out_views[w][b, j], in_=result[:])
+            tokens = slice(tile_index * P, (tile_index + 1) * P)
+            features = slice(h * BANK, (h + 1) * BANK)
+            bias = bias_all[w][:, features]
+            result = outs.tile([P, BANK], F32, tag="result")
+            acc = psum.tile([P, BANK], F32, tag="bank")
+            for g in range(PASSES):
+                nc.tensor.matmul_mx(
+                    out=acc[:],
+                    lhsT=xe_mx[0][:, g, tokens].bitcast(FP8X4),
+                    lhsT_scale=xe_mx[1][:, g, tokens],
+                    rhs=codes[:, g, features].bitcast(FP8X4),
+                    rhs_scale=scales[:, g, features],
+                    start=(g == 0),
+                    stop=(g == PASSES - 1),
+                )
+            if tile_index % 4 == 3 and (w, h, tile_index) != (2, 1, ROW_TILES - 1):
+                nc.scalar.copy(out=result[:], in_=acc[:])
+                nc.gpsimd.tensor_tensor(out=result[:], in0=result[:], in1=bias, op=ADD)
+            else:
+                nc.vector.tensor_tensor(out=result[:], in0=acc[:], in1=bias, op=ADD)
+            nc.sync.dma_start(out=out_views[w][b, j][:, features], in_=result[:])
 
         w_split = {}
 
-        def split_weight(copy, w, pair):
-            w_split[w, pair] = split_words(copy, weight_raw[w][pair])
+        def split_weight(index):
+            w, pair = divmod(index, PAIRS)
+            copy = nc.scalar.copy if index % 2 or index in (2, 4) else nc.vector.tensor_copy
+            w_split[index] = split_words(copy, weight_raw[w][pair])
+
+        def transpose_weight(index):
+            return transpose(w_split[index], split=True)
+
+        def quantise_weight(grouped, index):
+            w, pair = divmod(index, PAIRS)
+            quantise(grouped, pair, w_mx[w])
 
         w0 = transpose(w_embed_raw[0])
         w1 = transpose(w_embed_raw[1])
@@ -283,39 +285,33 @@ def tile_attention_pa_kernel(
         w2 = transpose(w_embed_raw[2])
         embed(0, 5)
         quantise(w2, 2, we_mx)
-        split_weight(nc.vector.tensor_copy, 0, 0)
+        split_weight(0)
         w3 = transpose(w_embed_raw[3])
         embed(0, 6)
         quantise(w3, 3, we_mx)
-        split_weight(nc.vector.tensor_copy, 0, 1)
+        split_weight(1)
         transpose_pos(1)
         embed(0, 7)
-        split_weight(nc.vector.tensor_copy, 0, 2)
-        for pair in range(PAIRS):
-            w_grouped = transpose(w_split[0, pair], split=True)
-            embed(1, 2 * pair)
-            embed(1, 2 * pair + 1)
-            quantise(w_grouped, pair, w_mx[0])
-            if pair == 0:
-                quantise_xe(0, 1)
-            if pair == 1:
-                quantise_xe(1, 0)
-            if pair == 0:
-                split_weight(nc.vector.tensor_copy, 0, 3)
-            elif pair < 3:
-                copy = nc.vector.tensor_copy if pair == 1 else nc.scalar.copy
-                split_weight(copy, 1, pair - 1)
+        for index in range(2):
+            w_grouped = transpose_weight(index)
+            embed(1, 2 * index)
+            embed(1, 2 * index + 1)
+            quantise_weight(w_grouped, index)
+            quantise_xe(index, 1 - index)
+            split_weight(index + 2)
+        for tile_index in range(4, ROW_TILES):
+            embed(1, tile_index)
         quantise_xe(1, 1)
 
-        for w in range(3):
+        index = 2
+        for half in range(6):
+            w, h = divmod(half, 2)
             for tile_index in range(ROW_TILES):
-                pair, second = divmod(tile_index, 2)
-                ahead = w < 2 and not second
-                if ahead:
-                    w_grouped = transpose(w_split[w + 1, pair], split=True)
-                project(w, tile_index)
-                if ahead:
-                    quantise(w_grouped, pair, w_mx[w + 1])
-                    after_next = (w + 1) * PAIRS + pair + 2
-                    if after_next < 3 * PAIRS:
-                        split_weight(nc.scalar.copy, *divmod(after_next, PAIRS))
+                if tile_index % 4 == 0 and index < 3 * PAIRS:
+                    w_grouped = transpose_weight(index)
+                project(w, h, tile_index)
+                if tile_index % 4 == 1 and index < 3 * PAIRS:
+                    quantise_weight(w_grouped, index)
+                    if index + 2 < 3 * PAIRS:
+                        split_weight(index + 2)
+                    index += 1

@@ -242,18 +242,14 @@ def tile_attention_pa_kernel(
                     start=(g == 0),
                     stop=(g == PASSES - 1),
                 )
-            if tile_index % 4 == 3 and (w, h, tile_index) != (2, 1, ROW_TILES - 1):
-                nc.scalar.copy(out=result[:], in_=acc[:])
-                nc.gpsimd.tensor_tensor(out=result[:], in0=result[:], in1=bias, op=ADD)
-            else:
-                nc.vector.tensor_tensor(out=result[:], in0=acc[:], in1=bias, op=ADD)
+            nc.vector.tensor_tensor(out=result[:], in0=acc[:], in1=bias, op=ADD)
             nc.sync.dma_start(out=out_views[w][b, j][:, features], in_=result[:])
 
         w_split = {}
 
         def split_weight(index):
             w, pair = divmod(index, PAIRS)
-            copy = nc.scalar.copy if index % 2 or index in (2, 4) else nc.vector.tensor_copy
+            copy = nc.scalar.copy if index else nc.vector.tensor_copy
             w_split[index] = split_words(copy, weight_raw[w][pair])
 
         def transpose_weight(index):
@@ -299,19 +295,27 @@ def tile_attention_pa_kernel(
             quantise_weight(w_grouped, index)
             quantise_xe(index, 1 - index)
             split_weight(index + 2)
-        for tile_index in range(4, ROW_TILES):
-            embed(1, tile_index)
+        embed(1, 4)
+        embed(1, 5)
+        w_grouped = transpose_weight(2)
+        embed(1, 6)
+        embed(1, 7)
         quantise_xe(1, 1)
+        quantise_weight(w_grouped, 2)
+        split_weight(4)
 
-        index = 2
+        ahead = {(0, 0): 3}
+        for index in range(4, 3 * PAIRS):
+            half, b = divmod(index - 2, 2)
+            ahead[half, b * LANE_TOKENS] = index
         for half in range(6):
             w, h = divmod(half, 2)
             for tile_index in range(ROW_TILES):
-                if tile_index % 4 == 0 and index < 3 * PAIRS:
+                if (half, tile_index) in ahead:
+                    index = ahead[half, tile_index]
                     w_grouped = transpose_weight(index)
                 project(w, h, tile_index)
-                if tile_index % 4 == 1 and index < 3 * PAIRS:
+                if (half, tile_index - 1) in ahead:
                     quantise_weight(w_grouped, index)
                     if index + 2 < 3 * PAIRS:
                         split_weight(index + 2)
-                    index += 1

from contextlib import ExitStack

import concourse.mybir as mybir
from concourse.masks import make_identity

BF16 = mybir.dt.bfloat16
F32 = mybir.dt.float32
U32 = mybir.dt.uint32
U8 = mybir.dt.uint8
FP8X4 = mybir.dt.float8_e4m3fn_x4
ADD = mybir.AluOpType.add
IDENTITY = mybir.ActivationFunctionType.Identity

P = 128
PACK = 4
K_PASS = P * PACK
E = 1024
PASSES = E // K_PASS
POSITIONS = 512
TOKENS = 2 * POSITIONS
ROW_TILES = 8
PAIRS = ROW_TILES // 2
WORDS = E // 2
BANK = 512
LANE_TOKENS = 4

FLOPS = 4 * 2 * TOKENS * E * E


def tile_attention_pa_kernel(
    tc, x, pos_embed, W_embed, b_embed, Wq, bq, Wk, bk, Wv, bv, out_0, out_1, out_2
):
    nc = tc.nc
    biases = (bq, bk, bv)

    x_view = x.rearrange("b (r j) s d -> b r (j s d)", j=LANE_TOKENS)
    pos_view = pos_embed.rearrange("(r j) e -> r j e", j=LANE_TOKENS)
    out_views = [
        out.rearrange("b (r j) h d -> b j r (h d)", j=LANE_TOKENS) for out in (out_0, out_1, out_2)
    ]
    w_embed_view = W_embed.rearrange("(g r t) k -> r g (t k)", r=P, t=PACK)
    weight_views = [w.rearrange("(i r) k -> r i k", r=P) for w in (Wq, Wk, Wv)]

    with ExitStack() as ctx:
        consts = ctx.enter_context(tc.tile_pool(name="consts", bufs=1))
        raws = ctx.enter_context(tc.tile_pool(name="raws", bufs=14))
        keep = ctx.enter_context(tc.tile_pool(name="keep", bufs=1))
        split = ctx.enter_context(tc.tile_pool(name="split", bufs=4))
        stage = ctx.enter_context(tc.tile_pool(name="stage", bufs=8))
        sums = ctx.enter_context(tc.tile_pool(name="sums", bufs=3))
        outs = ctx.enter_context(tc.tile_pool(name="outs", bufs=12))
        psum = ctx.enter_context(tc.psum_pool(name="psum", bufs=8))
        ctx.enter_context(tc.manual_schedule())

        ident = consts.tile([P, P], F32)
        make_identity(nc, ident[:])
        b_embed_bf = consts.tile([P, PASSES, PACK], BF16)
        nc.scalar.dma_start(
            out=b_embed_bf[:], in_=b_embed.rearrange("(g r t) -> r g t", r=P, t=PACK)
        )
        b_embed_f32 = consts.tile([P, ROW_TILES], F32)
        nc.scalar.activation(
            out=b_embed_f32[:], in_=b_embed_bf[:].rearrange("p g t -> p (g t)"), func=IDENTITY
        )

        def load_w_embed(pair):
            g, u = divmod(pair, 2)
            raw = raws.tile([P, 2 * E], BF16, tag="raw")
            nc.sync.dma_start(out=raw[:], in_=w_embed_view[:, g, 2 * u * E : 2 * (u + 1) * E])
            return raw

        def load_x(pair):
            b, half = divmod(pair, 2)
            raw = raws.tile([P, 2 * E], BF16, tag="raw")
            nc.sync.dma_start(out=raw[:], in_=x_view[b][:, 2 * half * E : 2 * (half + 1) * E])
            return raw

        def load_pos(g_out):
            raw = consts.tile([P, LANE_TOKENS, K_PASS], BF16, name="pos_raw_%d" % g_out)
            nc.sync.dma_start(
                out=raw[:], in_=pos_view[:, :, g_out * K_PASS : (g_out + 1) * K_PASS]
            )
            return raw

        def load_weight(w, pair):
            raw = raws.tile([P, 2 * E], BF16, tag="raw")
            nc.sync.dma_start(
                out=raw[:].rearrange("p (i k) -> p i k", i=2),
                in_=weight_views[w][:, 2 * pair : 2 * (pair + 1), :],
            )
            return raw

        bias_all = [consts.tile([P, E], BF16, name="bias_%d" % w) for w in range(3)]

        def load_bias(w):
            nc.sync.dma_start(out=bias_all[w][:], in_=biases[w].partition_broadcast(P))

        w_embed_raw = [load_w_embed(0), load_w_embed(1)]
        x_raw = [load_x(0)]
        pos_raw = [load_pos(0)]
        x_raw += [load_x(pair) for pair in (1, 2, 3)]
        w_embed_raw += [load_w_embed(2), load_w_embed(3)]
        pos_raw.append(load_pos(1))
        weight_raw = [[load_weight(0, 0), load_weight(0, 1)]]
        load_bias(0)
        weight_raw[0] += [load_weight(0, 2), load_weight(0, 3)]
        weight_raw += [[load_weight(w, pair) for pair in range(PAIRS)] for w in (1, 2)]
        load_bias(1)
        load_bias(2)

        def mx_operand(name):
            codes = keep.tile([P, PASSES, E], U32, name=name + "_codes", align_bytes=64)
            scales = keep.tile([P, PASSES, E], U8, name=name + "_scales", align_bytes=64)
            return codes, scales

        x_mx = mx_operand("x")
        we_mx = mx_operand("w_embed")
        xe_mx = mx_operand("xe")
        w_mx = [mx_operand(name) for name in ("wq", "wk", "wv")]

        def split_words(copy, raw):
            sorted_words = split.tile([P, 2 * E], BF16, tag="split", name="sorted_words")
            copy(
                out=sorted_words[:].bitcast(F32).rearrange("p (a u w) -> p a u w", a=4, u=2),
                in_=raw[:].bitcast(F32).rearrange("p (a w u) -> p a u w", a=4, u=2),
            )
            return sorted_words

        def transpose(raw, split=False):
            words = raw[:].bitcast(F32)
            grouped_tiles = []
            for g in range(PASSES):
                bank = psum.tile([P, 2, 2, P], F32, tag="bank")
                for i in range(2):
                    for u in range(2):
                        if split:
                            first_word = i * WORDS + (2 * g + u) * P
                            block = words[:, first_word : first_word + P]
                        else:
                            first_word = i * WORDS + 2 * g * P + u
                            block = words[:, first_word : first_word + 2 * P - 1 : 2]
                        nc.tensor.transpose(bank[:, i, u, :], block, ident[:])
                grouped = stage.tile([P, 2 * P * PACK], BF16, tag="grouped", align_bytes=64)
                nc.scalar.copy(
                    out=grouped[:].bitcast(F32).rearrange("p (i r u) -> p i r u", i=2, u=2),
                    in_=bank[:].rearrange("p i u r -> p i r u"),
                )
                grouped_tiles.append(grouped)
            return grouped_tiles

        def quantise(grouped_tiles, pair, operand):
            cols = slice(2 * pair * P, 2 * (pair + 1) * P)
            for g in range(PASSES):
                nc.vector.quantize_mx(
                    out=operand[0][:, g, cols].bitcast(FP8X4),
                    scales=operand[1][:, g, cols],
                    in_=grouped_tiles[g][:],
                )

        pos_planes = [
            consts.tile([P, PACK, POSITIONS], F32, name="pos_planes_%d" % g) for g in range(PASSES)
        ]

        def transpose_pos(g_out):
            for u in range(2):
                bank = psum.tile([P, LANE_TOKENS, P], F32, tag="bank")
                for j in range(LANE_TOKENS):
                    nc.tensor.transpose(
                        bank[:, j, :], pos_raw[g_out][:, j, :].bitcast(F32)[:, u : 2 * P : 2], ident[:]
                    )
                pairs = (
                    bank[:]
                    .rearrange("p j r -> p (j r)")
                    .bitcast(BF16)
                    .rearrange("p (c e) -> p c e", e=2)
                )
                for e in range(2):
                    t = 2 * u + e
                    feature_tile = PACK * g_out + t
                    nc.scalar.activation(
                        out=pos_planes[g_out][:, t, :],
                        in_=pairs[:, :, e],
                        func=IDENTITY,
                        bias=b_embed_f32[:, feature_tile : feature_tile + 1],
                        scale=1.0,
                    )

        xe_sums = {}

        def embed(g_out, tile_index):
            b, j = divmod(tile_index, LANE_TOKENS)
            if j == 0:
                xe_sums[g_out, b] = sums.tile(
                    [P, POSITIONS * PACK], BF16, tag="xe_sum", name="xe_sum", align_bytes=64
                )
            tokens = slice(tile_index * P, (tile_index + 1) * P)
            acc = psum.tile([P, PACK, P], F32, tag="bank")
            for t in range(PACK):
                features = slice((PACK * g_out + t) * P, (PACK * g_out + t + 1) * P)
                for g in range(PASSES):
                    nc.tensor.matmul_mx(
                        out=acc[:, t, :],
                        lhsT=we_mx[0][:, g, features].bitcast(FP8X4),
                        lhsT_scale=we_mx[1][:, g, features],
                        rhs=x_mx[0][:, g, tokens].bitcast(FP8X4),
                        rhs_scale=x_mx[1][:, g, tokens],
                        start=(g == 0),
                        stop=(g == PASSES - 1),
                    )
            nc.vector.tensor_tensor(
                out=xe_sums[g_out, b][:, j * P * PACK : (j + 1) * P * PACK].rearrange(
                    "p (r t) -> p r t", t=PACK
                ),
                in0=acc[:].rearrange("p t r -> p r t"),
                in1=pos_planes[g_out][:, :, j * P : (j + 1) * P].rearrange("p t r -> p r t"),
                op=ADD,
            )

        def quantise_xe(g_out, b):
            batch = slice(b * POSITIONS, (b + 1) * POSITIONS)
            nc.vector.quantize_mx(
                out=xe_mx[0][:, g_out, batch].bitcast(FP8X4),
                scales=xe_mx[1][:, g_out, batch],
                in_=xe_sums[g_out, b][:],
            )

        def project(w, h, tile_index):
            codes, scales = w_mx[w]
            b, j = divmod(tile_index, LANE_TOKENS)
            tokens = slice(tile_index * P, (tile_index + 1) * P)
            features = slice(h * BANK, (h + 1) * BANK)
            bias = bias_all[w][:, features]
            result = outs.tile([P, BANK], F32, tag="result")
            acc = psum.tile([P, BANK], F32, tag="bank")
            for g in range(PASSES):
                nc.tensor.matmul_mx(
                    out=acc[:],
                    lhsT=xe_mx[0][:, g, tokens].bitcast(FP8X4),
                    lhsT_scale=xe_mx[1][:, g, tokens],
                    rhs=codes[:, g, features].bitcast(FP8X4),
                    rhs_scale=scales[:, g, features],
                    start=(g == 0),
                    stop=(g == PASSES - 1),
                )
            nc.vector.tensor_tensor(out=result[:], in0=acc[:], in1=bias, op=ADD)
            nc.sync.dma_start(out=out_views[w][b, j][:, features], in_=result[:])

        w_split = {}

        def split_weight(index):
            w, pair = divmod(index, PAIRS)
            copy = nc.scalar.copy if index else nc.vector.tensor_copy
            w_split[index] = split_words(copy, weight_raw[w][pair])

        def transpose_weight(index):
            return transpose(w_split[index], split=True)

        def quantise_weight(grouped, index):
            w, pair = divmod(index, PAIRS)
            quantise(grouped, pair, w_mx[w])

        w0 = transpose(w_embed_raw[0])
        w1 = transpose(w_embed_raw[1])
        quantise(w0, 0, we_mx)
        x0 = transpose(x_raw[0])
        quantise(w1, 1, we_mx)
        transpose_pos(0)
        quantise(x0, 0, x_mx)
        x1 = transpose(x_raw[1])
        embed(0, 0)
        quantise(x1, 1, x_mx)
        x2 = transpose(x_raw[2])
        embed(0, 1)
        embed(0, 2)
        quantise(x2, 2, x_mx)
        x3 = transpose(x_raw[3])
        embed(0, 3)
        embed(0, 4)
        quantise(x3, 3, x_mx)
        quantise_xe(0, 0)
        w2 = transpose(w_embed_raw[2])
        embed(0, 5)
        quantise(w2, 2, we_mx)
        split_weight(0)
        w3 = transpose(w_embed_raw[3])
        embed(0, 6)
        quantise(w3, 3, we_mx)
        split_weight(1)
        transpose_pos(1)
        embed(0, 7)
        for index in range(2):
            w_grouped = transpose_weight(index)
            embed(1, 2 * index)
            embed(1, 2 * index + 1)
            quantise_weight(w_grouped, index)
            quantise_xe(index, 1 - index)
            split_weight(index + 2)
        embed(1, 4)
        embed(1, 5)
        w_grouped = transpose_weight(2)
        embed(1, 6)
        embed(1, 7)
        quantise_xe(1, 1)
        quantise_weight(w_grouped, 2)
        split_weight(4)

        ahead = {(0, 0): 3}
        for index in range(4, 3 * PAIRS):
            half, b = divmod(index - 2, 2)
            ahead[half, b * LANE_TOKENS] = index
        for half in range(6):
            w, h = divmod(half, 2)
            for tile_index in range(ROW_TILES):
                if (half, tile_index) in ahead:
                    index = ahead[half, tile_index]
                    w_grouped = transpose_weight(index)
                project(w, h, tile_index)
                if (half, tile_index - 1) in ahead:
                    quantise_weight(w_grouped, index)
                    if index + 2 < 3 * PAIRS:
                        split_weight(index + 2)
